import numpy as np
import ml_dtypes


def mxq(x, axis, fmt="e4m3"):
    dtype, down = {"e4m3": (ml_dtypes.float8_e4m3fn, 7), "e5m2": (ml_dtypes.float8_e5m2, 14)}[fmt]
    v = np.moveaxis(np.asarray(x, np.float32).astype(ml_dtypes.bfloat16).astype(np.float64), axis, -1)
    blocks = v.reshape(v.shape[:-1] + (-1, 32))
    amax = np.abs(blocks).max(-1, keepdims=True)
    byte = np.maximum(np.where(amax > 0, np.frexp(amax)[1] - 1 + 127, 0) - down, 1)
    scale = np.exp2(byte - 127.0)
    codes = (blocks / scale).astype(np.float32).astype(dtype).astype(np.float64)
    return np.moveaxis((codes * scale).reshape(v.shape), -1, axis)


WIDE = False


def mx_kscale(k):
    if not WIDE:
        return np.ones(k)
    levels = np.array([10, -10, 5, -5, 0])
    a = np.random.permutation(np.resize(levels, k // 512 * 4)).reshape(k // 512, 4)
    idx = np.arange(k)
    return np.exp2(a[idx // 512, idx % 128 // 32])


BF16 = ml_dtypes.bfloat16


def bf(x):
    return np.asarray(x, np.float32).astype(BF16)


def f64(x):
    return np.asarray(x).astype(np.float64)


B, S, D, DI = 4, 512, 512, 2048
EPS = 1e-12
KV_RMS = np.sqrt(S * (S / D + 1.0) / DI)


def l2norm(v):
    n = np.sqrt(np.sum(v * v, axis=-1, keepdims=True))
    return v / np.maximum(n, EPS)


def setup_inputs():
    t = mx_kscale(DI)
    return {"x": bf(np.random.standard_normal((B, S, D))),
            "wq": bf(np.random.standard_normal((D, DI)) / np.sqrt(D)),
            "kv": bf(np.random.standard_normal((B, 1, DI)) * KV_RMS * t),
            "wo": bf(np.random.standard_normal((DI, D)) / KV_RMS / t[:, None])}


def reference(x, wq, kv, wo):
    xf = f64(x)
    q = l2norm(mxq(xf, 2, "e4m3") @ mxq(f64(wq), 0, "e4m3"))
    g = q * f64(kv)
    return (mxq(g, 2, "e4m3") @ mxq(f64(wo), 0, "e4m3")) + xf

@@ -1,0 +1,317 @@
+from contextlib import ExitStack
+
+import concourse.mybir as mybir
+from concourse.masks import make_identity
+
+F32 = mybir.dt.float32
+BF16 = mybir.dt.bfloat16
+U32 = mybir.dt.uint32
+U8 = mybir.dt.uint8
+FP8X4 = mybir.dt.float8_e4m3fn_x4
+MULT = mybir.AluOpType.mult
+ADD = mybir.AluOpType.add
+ACT = mybir.ActivationFunctionType
+
+P = 128
+PACK = 4
+K_PASS = P * PACK
+BATCH, TOKENS, D_MODEL, D_INNER = 4, 512, 512, 2048
+TOKEN_TILES = TOKENS // P
+ALL_TILES = BATCH * TOKEN_TILES
+CHUNKS = D_INNER // K_PASS
+FEATURE_TILES = D_INNER // P
+GROUPS = BATCH * CHUNKS
+STEPS = GROUPS * PACK
+EPS = 1e-12
+
+NORM_LEAD = TOKEN_TILES + 1
+OUT_LAG = STEPS // BATCH + PACK + 1
+SCALAR_COLS = TOKENS // 4
+
+FLOPS = 2 * BATCH * TOKENS * D_MODEL * D_INNER * 2
+
+
+def side_by_side(planes):
+    return planes.rearrange("p t (c i) -> p c t i", i=4)
+
+
+def interleaved(grouped):
+    return grouped.rearrange("p (c i) t -> p c t i", i=4)
+
+
+def tile_hydraencoderlayer_pb_kernel(tc, x, wq, kv, wo, out):
+    nc = tc.nc
+    with ExitStack() as ctx:
+        keep = ctx.enter_context(tc.tile_pool(name="keep", bufs=1))
+        raw_pool = ctx.enter_context(tc.tile_pool(name="raw", bufs=2 * CHUNKS))
+        wo_pool = ctx.enter_context(tc.tile_pool(name="wo_grouped", bufs=CHUNKS))
+        stage = ctx.enter_context(tc.tile_pool(name="stage", bufs=3))
+        code_pool = ctx.enter_context(tc.tile_pool(name="g_codes", bufs=2 * CHUNKS))
+        junk_pool = ctx.enter_context(tc.tile_pool(name="junk", bufs=4))
+        small = ctx.enter_context(tc.tile_pool(name="small", bufs=2))
+        store_pool = ctx.enter_context(tc.tile_pool(name="store", bufs=4))
+        psum_val = ctx.enter_context(tc.psum_pool(name="psum_val", bufs=3))
+        psum_norm = ctx.enter_context(tc.psum_pool(name="psum_norm", bufs=3))
+        psum_out = ctx.enter_context(tc.psum_pool(name="psum_out", bufs=2))
+        ctx.enter_context(tc.manual_schedule())
+
+        ident_f32 = keep.tile([P, P], F32)
+        make_identity(nc, ident_f32[:])
+        ident_bf16 = keep.tile([P, P], BF16)
+        make_identity(nc, ident_bf16[:])
+        warm = keep.tile([P, 1], F32)
+        nc.vector.memset(warm[:], 1.0)
+        nc.scalar.activation(out=warm[:], in_=warm[:], func=ACT.Sqrt)
+
+        x_sb = keep.tile([P, ALL_TILES, D_MODEL], BF16)
+        x_codes = keep.tile([P, BATCH, TOKENS], U32, align_bytes=64)
+        x_scales = keep.tile([P, BATCH, TOKENS], U8, align_bytes=64)
+        wq_codes = keep.tile([P, D_INNER], U32, align_bytes=64)
+        wq_scales = keep.tile([P, D_INNER], U8, align_bytes=64)
+        wo_codes = keep.tile([P, CHUNKS, D_MODEL], U32, align_bytes=64)
+        wo_scales = keep.tile([P, CHUNKS, D_MODEL], U8, align_bytes=64)
+        kv_rows = keep.tile([P, P], BF16)
+        kv_cols = keep.tile([P, BATCH * FEATURE_TILES], F32)
+        sumsq = keep.tile([P, ALL_TILES, CHUNKS], F32)
+
+        wq_raw = []
+        for i in range(BATCH):
+            nc.sync.dma_start(
+                out=x_sb[:, i * TOKEN_TILES : (i + 1) * TOKEN_TILES, :],
+                in_=x[i].rearrange("(m p) d -> p m d", p=P),
+            )
+            raw = raw_pool.tile([P, PACK, K_PASS], BF16, tag="raw")
+            for u in range(2):
+                nc.sync.dma_start(
+                    out=raw[:, 2 * u : 2 * u + 2, :],
+                    in_=wq[2 * P * u : 2 * P * (u + 1), i * K_PASS : (i + 1) * K_PASS].rearrange(
+                        "(p e) c -> p e c", e=2
+                    ),
+                )
+            wq_raw.append(raw)
+        wo_raw = []
+        wo_view = wo.rearrange("(c t p) n -> c p t n", t=PACK, p=P)
+        for c in range(CHUNKS):
+            raw = raw_pool.tile([P, PACK, D_MODEL], BF16, tag="raw")
+            nc.sync.dma_start(out=raw[:], in_=wo_view[c])
+            wo_raw.append(raw)
+        nc.vector.memset(kv_rows[:], 0.0)
+        nc.scalar.dma_start(
+            out=kv_rows[0 : BATCH * FEATURE_TILES, :], in_=kv.rearrange("b o (j p) -> (b o j) p", p=P)
+        )
+
+        x_words = x_sb[:].bitcast(F32)
+
+        def transpose_x(b, psum_pool, tag):
+            banks = []
+            for h in range(2):
+                xt = psum_pool.tile([P, 2, 2, P], F32, tag=tag)
+                for m in range(2):
+                    for u in range(2):
+                        nc.tensor.transpose(
+                            xt[:, m, u, :],
+                            x_words[:, b * TOKEN_TILES + 2 * h + m, u * P : (u + 1) * P],
+                            ident_f32[:],
+                        )
+                banks.append(xt)
+            return banks
+
+        def gather_x(banks, copy):
+            xg = stage.tile([P, TOKENS, PACK], BF16, tag="xg", align_bytes=64)
+            xg_words = xg[:].bitcast(F32)
+            for h in range(2):
+                copy(
+                    out=xg_words[:, 2 * P * h : 2 * P * (h + 1), :].rearrange("p (m r) u -> p m r u", m=2),
+                    in_=banks[h][:].rearrange("p m u r -> p m r u"),
+                )
+            return xg
+
+        def quantise(grouped, codes, scales):
+            nc.vector.quantize_mx(
+                out=codes.bitcast(FP8X4), scales=scales, in_=grouped[:].rearrange("p w j -> p (w j)")
+            )
+
+        def gpsimd_regroup(grouped_cols, plane_cols):
+            nc.gpsimd.tensor_scalar(
+                out=grouped_cols,
+                in0=plane_cols.rearrange("p t w -> p w t"),
+                scalar1=1.0,
+                scalar2=0.0,
+                op0=MULT,
+                op1=ADD,
+            )
+
+        def regroup_wq(c):
+            wg = stage.tile([P, K_PASS, PACK], BF16, tag="wg", align_bytes=64)
+            nc.vector.tensor_copy(out=interleaved(wg[:]), in_=side_by_side(wq_raw[c][:]))
+            return wg
+
+        def quantise_wq(c, wg):
+            cols = slice(c * K_PASS, (c + 1) * K_PASS)
+            quantise(wg, wq_codes[:, cols], wq_scales[:, cols])
+
+        def norm_pass(tile, c):
+            b, m = divmod(tile, TOKEN_TILES)
+            tokens = slice(m * P, (m + 1) * P)
+            cols = slice(c * K_PASS, (c + 1) * K_PASS)
+            a_tok = psum_norm.tile([P, K_PASS], F32, tag="norm")
+            nc.tensor.matmul_mx(
+                out=a_tok[:],
+                lhsT=x_codes[:, b, tokens].bitcast(FP8X4),
+                lhsT_scale=x_scales[:, b, tokens],
+                rhs=wq_codes[:, cols].bitcast(FP8X4),
+                rhs_scale=wq_scales[:, cols],
+                start=True,
+                stop=True,
+            )
+            squares = junk_pool.tile([P, K_PASS], BF16)
+            nc.scalar.activation(
+                out=squares[:], in_=a_tok[:], func=ACT.Square, accum_out=sumsq[:, tile, c : c + 1]
+            )
+
+        inv_norm = {}
+
+        def inverse_norms(b):
+            tiles = slice(b * TOKEN_TILES, (b + 1) * TOKEN_TILES)
+            n2 = small.tile([P, TOKEN_TILES], F32)
+            nc.vector.tensor_reduce(out=n2[:], in_=sumsq[:, tiles, :], axis=mybir.AxisListType.X, op=ADD)
+            floored = small.tile([P, TOKEN_TILES], F32)
+            nc.vector.tensor_scalar_max(out=floored[:], in0=n2[:], scalar1=EPS * EPS)
+            norm = small.tile([P, TOKEN_TILES], F32)
+            nc.scalar.activation(out=norm[:], in_=floored[:], func=ACT.Sqrt)
+            rn = small.tile([P, TOKEN_TILES], F32)
+            nc.vector.reciprocal(out=rn[:], in_=norm[:])
+            spread = psum_norm.tile([P, TOKENS], F32, tag="norm")
+            for m in range(TOKEN_TILES):
+                nc.tensor.transpose(
+                    spread[:, m * P : (m + 1) * P], rn[:, m : m + 1].to_broadcast([P, P]), ident_f32[:]
+                )
+            rn_all = small.tile([P, TOKENS], F32)
+            nc.scalar.copy(out=rn_all[:], in_=spread[:])
+            inv_norm[b] = rn_all
+
+        planes = {}
+
+        def value_pass(s, t):
+            b, c = divmod(s, CHUNKS)
+            j = PACK * c + t
+            feats = slice(j * P, (j + 1) * P)
+            if t == 0:
+                new_planes = stage.tile([P, PACK, TOKENS], BF16, tag="planes")
+                planes[s] = new_planes
+            a_feat = psum_val.tile([P, TOKENS], F32, tag="val")
+            nc.tensor.matmul_mx(
+                out=a_feat[:],
+                lhsT=wq_codes[:, feats].bitcast(FP8X4),
+                lhsT_scale=wq_scales[:, feats],
+                rhs=x_codes[:, b, :].bitcast(FP8X4),
+                rhs_scale=x_scales[:, b, :],
+                start=True,
+                stop=True,
+            )
+            col = b * FEATURE_TILES + j
+            nc.vector.scalar_tensor_tensor(
+                out=planes[s][:, t, :],
+                in0=a_feat[:],
+                scalar=kv_cols[:, col : col + 1],
+                in1=inv_norm[b][:],
+                op0=MULT,
+                op1=MULT,
+            )
+
+        grouped = {}
+
+        def regroup_g(s):
+            gg = stage.tile([P, TOKENS, PACK], BF16, tag="gg", align_bytes=64)
+            gpsimd_regroup(gg[:, SCALAR_COLS:TOKENS, :], planes[s][:, :, SCALAR_COLS:TOKENS])
+            nc.scalar.copy(
+                out=interleaved(gg[:, 0:SCALAR_COLS, :]), in_=side_by_side(planes[s][:, :, 0:SCALAR_COLS])
+            )
+            grouped[s] = gg
+
+        g_codes = {}
+        g_scales = {}
+
+        def quantise_g(s):
+            codes = code_pool.tile([P, TOKENS], U32, tag="codes", align_bytes=64)
+            scales = code_pool.tile([P, TOKENS], U8, tag="scales", align_bytes=64)
+            quantise(grouped[s], codes[:], scales[:])
+            g_codes[s] = codes
+            g_scales[s] = scales
+
+        acc = {}
+
+        def out_pass(b, m, c):
+            s = b * CHUNKS + c
+            tokens = slice(m * P, (m + 1) * P)
+            if c == 0:
+                bank = psum_out.tile([P, D_MODEL], F32, tag="out")
+                acc[m] = bank
+            nc.tensor.matmul_mx(
+                out=acc[m][:],
+                lhsT=g_codes[s][:, tokens].bitcast(FP8X4),
+                lhsT_scale=g_scales[s][:, tokens],
+                rhs=wo_codes[:, c, :].bitcast(FP8X4),
+                rhs_scale=wo_scales[:, c, :],
+                start=(c == 0),
+                stop=(c == CHUNKS - 1),
+            )
+
+        def add_x_and_store(b, m):
+            result = store_pool.tile([P, D_MODEL], F32)
+            nc.vector.tensor_tensor(
+                out=result[:], in0=acc[m][:], in1=x_sb[:, b * TOKEN_TILES + m, :], op=ADD
+            )
+            nc.sync.dma_start(out=out[b, m * P : (m + 1) * P, :], in_=result[:])
+
+        x_banks = {0: transpose_x(0, psum_val, "val")}
+        xg = gather_x(x_banks[0], nc.scalar.copy)
+        wg = regroup_wq(0)
+        quantise(xg, x_codes[:, 0, :], x_scales[:, 0, :])
+        quantise_wq(0, wg)
+        kv_ps = psum_norm.tile([P, P], BF16, tag="norm")
+        nc.tensor.transpose(kv_ps[:], kv_rows[:], ident_bf16[:])
+        nc.vector.tensor_copy(out=kv_cols[:], in_=kv_ps[:, 0 : BATCH * FEATURE_TILES])
+        wo_grouped = []
+        for c in range(CHUNKS):
+            wog = wo_pool.tile([P, D_MODEL, PACK], BF16, align_bytes=64)
+            gpsimd_regroup(wog[:], wo_raw[c][:])
+            wo_grouped.append(wog)
+        for c in range(CHUNKS):
+            for tile in range(TOKEN_TILES):
+                norm_pass(tile, c)
+            if c + 1 < CHUNKS:
+                quantise_wq(c + 1, regroup_wq(c + 1))
+            if c == 0:
+                x_banks[1] = transpose_x(1, psum_out, "out")
+            if c == 1:
+                x_banks[2] = transpose_x(2, psum_val, "val")
+        for b in range(1, BATCH):
+            if b == BATCH - 1:
+                x_banks[b] = transpose_x(b, psum_val, "val")
+            quantise(gather_x(x_banks[b], nc.vector.tensor_copy), x_codes[:, b, :], x_scales[:, b, :])
+        inverse_norms(0)
+
+        for k in range(STEPS + OUT_LAG):
+            s, t = divmod(k, PACK)
+            if t == 0 and 1 <= s <= CHUNKS:
+                quantise(wo_grouped[s - 1], wo_codes[:, s - 1, :], wo_scales[:, s - 1, :])
+            if s < GROUPS:
+                value_pass(s, t)
+                first_tile = TOKEN_TILES if s == 0 else s + NORM_LEAD
+                for tile in range(first_tile, min(s + NORM_LEAD + 1, ALL_TILES)):
+                    norm_pass(tile, t)
+            if k >= OUT_LAG:
+                b, rest = divmod(k - OUT_LAG, TOKEN_TILES * CHUNKS)
+                m, c = divmod(rest, CHUNKS)
+                out_pass(b, m, c)
+                if c == CHUNKS - 1:
+                    add_x_and_store(b, m)
+            if t == PACK - 1:
+                if s < GROUPS:
+                    regroup_g(s)
+                    last_tile = s + NORM_LEAD
+                    if last_tile < ALL_TILES and last_tile % TOKEN_TILES == TOKEN_TILES - 1:
+                        inverse_norms(last_tile // TOKEN_TILES)
+                if 1 <= s <= GROUPS:
+                    quantise_g(s - 1)

@@ -27,6 +27,8 @@ EPS = 1e-12
 NORM_LEAD = TOKEN_TILES + 1
 OUT_LAG = STEPS // BATCH + PACK + 1
 SCALAR_COLS = TOKENS // 4
+NORMS_AFTER = 1
+SPREAD_AFTER = 3
 
 FLOPS = 2 * BATCH * TOKENS * D_MODEL * D_INNER * 2
 
@@ -44,7 +46,6 @@ def tile_hydraencoderlayer_pb_kernel(tc, x, wq, kv, wo, out):
     with ExitStack() as ctx:
         keep = ctx.enter_context(tc.tile_pool(name="keep", bufs=1))
         raw_pool = ctx.enter_context(tc.tile_pool(name="raw", bufs=2 * CHUNKS))
-        wo_pool = ctx.enter_context(tc.tile_pool(name="wo_grouped", bufs=CHUNKS))
         stage = ctx.enter_context(tc.tile_pool(name="stage", bufs=3))
         code_pool = ctx.enter_context(tc.tile_pool(name="g_codes", bufs=2 * CHUNKS))
         junk_pool = ctx.enter_context(tc.tile_pool(name="junk", bufs=4))
@@ -74,27 +75,33 @@ def tile_hydraencoderlayer_pb_kernel(tc, x, wq, kv, wo, out):
         kv_cols = keep.tile([P, BATCH * FEATURE_TILES], F32)
         sumsq = keep.tile([P, ALL_TILES, CHUNKS], F32)
 
-        wq_raw = []
-        for i in range(BATCH):
+        def load_x(b):
             nc.sync.dma_start(
-                out=x_sb[:, i * TOKEN_TILES : (i + 1) * TOKEN_TILES, :],
-                in_=x[i].rearrange("(m p) d -> p m d", p=P),
+                out=x_sb[:, b * TOKEN_TILES : (b + 1) * TOKEN_TILES, :],
+                in_=x[b].rearrange("(m p) d -> p m d", p=P),
             )
+
+        load_x(0)
+        wq_raw = []
+        for c in range(CHUNKS):
             raw = raw_pool.tile([P, PACK, K_PASS], BF16, tag="raw")
             for u in range(2):
                 nc.sync.dma_start(
                     out=raw[:, 2 * u : 2 * u + 2, :],
-                    in_=wq[2 * P * u : 2 * P * (u + 1), i * K_PASS : (i + 1) * K_PASS].rearrange(
+                    in_=wq[2 * P * u : 2 * P * (u + 1), c * K_PASS : (c + 1) * K_PASS].rearrange(
                         "(p e) c -> p e c", e=2
                     ),
                 )
             wq_raw.append(raw)
+        load_x(1)
         wo_raw = []
         wo_view = wo.rearrange("(c t p) n -> c p t n", t=PACK, p=P)
         for c in range(CHUNKS):
             raw = raw_pool.tile([P, PACK, D_MODEL], BF16, tag="raw")
             nc.sync.dma_start(out=raw[:], in_=wo_view[c])
             wo_raw.append(raw)
+        load_x(2)
+        load_x(3)
         nc.vector.memset(kv_rows[:], 0.0)
         nc.scalar.dma_start(
             out=kv_rows[0 : BATCH * FEATURE_TILES, :], in_=kv.rearrange("b o (j p) -> (b o j) p", p=P)
@@ -141,14 +148,17 @@ def tile_hydraencoderlayer_pb_kernel(tc, x, wq, kv, wo, out):
                 op1=ADD,
             )
 
-        def regroup_wq(c):
+        def regroup_weight(raw):
             wg = stage.tile([P, K_PASS, PACK], BF16, tag="wg", align_bytes=64)
-            nc.vector.tensor_copy(out=interleaved(wg[:]), in_=side_by_side(wq_raw[c][:]))
+            nc.vector.tensor_copy(out=interleaved(wg[:]), in_=side_by_side(raw[:]))
             return wg
 
         def quantise_wq(c, wg):
             cols = slice(c * K_PASS, (c + 1) * K_PASS)
             quantise(wg, wq_codes[:, cols], wq_scales[:, cols])
+
+        def prepare_wo(c):
+            quantise(regroup_weight(wo_raw[c]), wo_codes[:, c, :], wo_scales[:, c, :])
 
         def norm_pass(tile, c):
             b, m = divmod(tile, TOKEN_TILES)
@@ -169,18 +179,22 @@ def tile_hydraencoderlayer_pb_kernel(tc, x, wq, kv, wo, out):
                 out=squares[:], in_=a_tok[:], func=ACT.Square, accum_out=sumsq[:, tile, c : c + 1]
             )
 
+        norms = {}
         inv_norm = {}
 
-        def inverse_norms(b):
+        def floored_norms(b):
             tiles = slice(b * TOKEN_TILES, (b + 1) * TOKEN_TILES)
             n2 = small.tile([P, TOKEN_TILES], F32)
             nc.vector.tensor_reduce(out=n2[:], in_=sumsq[:, tiles, :], axis=mybir.AxisListType.X, op=ADD)
-            floored = small.tile([P, TOKEN_TILES], F32)
-            nc.vector.tensor_scalar_max(out=floored[:], in0=n2[:], scalar1=EPS * EPS)
+            excess = small.tile([P, TOKEN_TILES], F32)
+            nc.scalar.activation(out=excess[:], in_=n2[:], func=ACT.Relu, bias=-EPS * EPS)
             norm = small.tile([P, TOKEN_TILES], F32)
-            nc.scalar.activation(out=norm[:], in_=floored[:], func=ACT.Sqrt)
+            nc.scalar.activation(out=norm[:], in_=excess[:], func=ACT.Sqrt, bias=EPS * EPS)
+            norms[b] = norm
+
+        def spread_inverse_norms(b):
             rn = small.tile([P, TOKEN_TILES], F32)
-            nc.vector.reciprocal(out=rn[:], in_=norm[:])
+            nc.vector.reciprocal(out=rn[:], in_=norms[b][:])
             spread = psum_norm.tile([P, TOKENS], F32, tag="norm")
             for m in range(TOKEN_TILES):
                 nc.tensor.transpose(
@@ -266,36 +280,32 @@ def tile_hydraencoderlayer_pb_kernel(tc, x, wq, kv, wo, out):
 
         x_banks = {0: transpose_x(0, psum_val, "val")}
         xg = gather_x(x_banks[0], nc.scalar.copy)
-        wg = regroup_wq(0)
+        wg = regroup_weight(wq_raw[0])
         quantise(xg, x_codes[:, 0, :], x_scales[:, 0, :])
         quantise_wq(0, wg)
         kv_ps = psum_norm.tile([P, P], BF16, tag="norm")
         nc.tensor.transpose(kv_ps[:], kv_rows[:], ident_bf16[:])
         nc.vector.tensor_copy(out=kv_cols[:], in_=kv_ps[:, 0 : BATCH * FEATURE_TILES])
-        wo_grouped = []
-        for c in range(CHUNKS):
-            wog = wo_pool.tile([P, D_MODEL, PACK], BF16, align_bytes=64)
-            gpsimd_regroup(wog[:], wo_raw[c][:])
-            wo_grouped.append(wog)
         for c in range(CHUNKS):
             for tile in range(TOKEN_TILES):
                 norm_pass(tile, c)
             if c + 1 < CHUNKS:
-                quantise_wq(c + 1, regroup_wq(c + 1))
-            if c == 0:
-                x_banks[1] = transpose_x(1, psum_out, "out")
+                quantise_wq(c + 1, regroup_weight(wq_raw[c + 1]))
             if c == 1:
-                x_banks[2] = transpose_x(2, psum_val, "val")
-        for b in range(1, BATCH):
-            if b == BATCH - 1:
-                x_banks[b] = transpose_x(b, psum_val, "val")
-            quantise(gather_x(x_banks[b], nc.vector.tensor_copy), x_codes[:, b, :], x_scales[:, b, :])
-        inverse_norms(0)
+                x_banks[1] = transpose_x(1, psum_val, "val")
+        quantise(gather_x(x_banks[1], nc.vector.tensor_copy), x_codes[:, 1, :], x_scales[:, 1, :])
+        prepare_wo(0)
+        prepare_wo(1)
+        floored_norms(0)
+        prepare_wo(2)
+        spread_inverse_norms(0)
+        prepare_wo(3)
 
         for k in range(STEPS + OUT_LAG):
             s, t = divmod(k, PACK)
-            if t == 0 and 1 <= s <= CHUNKS:
-                quantise(wo_grouped[s - 1], wo_codes[:, s - 1, :], wo_scales[:, s - 1, :])
+            late_x = s + 2 if s + 2 < BATCH else None
+            if late_x is not None and t == 0:
+                x_banks[late_x] = transpose_x(late_x, psum_out, "out")
             if s < GROUPS:
                 value_pass(s, t)
                 first_tile = TOKEN_TILES if s == 0 else s + NORM_LEAD
@@ -307,11 +317,18 @@ def tile_hydraencoderlayer_pb_kernel(tc, x, wq, kv, wo, out):
                 out_pass(b, m, c)
                 if c == CHUNKS - 1:
                     add_x_and_store(b, m)
+            for b in range(1, BATCH):
+                last_norm_step = PACK * (TOKEN_TILES * (b + 1) - 1 - NORM_LEAD) + PACK - 1
+                if k == last_norm_step + NORMS_AFTER:
+                    floored_norms(b)
+                if k == last_norm_step + SPREAD_AFTER:
+                    spread_inverse_norms(b)
+            if late_x is not None and t == PACK - 2:
+                late_xg = gather_x(x_banks[late_x], nc.vector.tensor_copy)
             if t == PACK - 1:
                 if s < GROUPS:
                     regroup_g(s)
-                    last_tile = s + NORM_LEAD
-                    if last_tile < ALL_TILES and last_tile % TOKEN_TILES == TOKEN_TILES - 1:
-                        inverse_norms(last_tile // TOKEN_TILES)
                 if 1 <= s <= GROUPS:
                     quantise_g(s - 1)
+                if late_x is not None:
+                    quantise(late_xg, x_codes[:, late_x, :], x_scales[:, late_x, :])

@@ -29,6 +29,7 @@ OUT_LAG = STEPS // BATCH + PACK + 1
 SCALAR_COLS = TOKENS // 4
 NORMS_AFTER = 1
 SPREAD_AFTER = 3
+SQUARES_DONE = PACK * (ALL_TILES - NORM_LEAD)
 
 FLOPS = 2 * BATCH * TOKENS * D_MODEL * D_INNER * 2
 
@@ -235,11 +236,12 @@ def tile_hydraencoderlayer_pb_kernel(tc, x, wq, kv, wo, out):
 
         grouped = {}
 
-        def regroup_g(s):
+        def regroup_g(s, scalar_cols):
             gg = stage.tile([P, TOKENS, PACK], BF16, tag="gg", align_bytes=64)
-            gpsimd_regroup(gg[:, SCALAR_COLS:TOKENS, :], planes[s][:, :, SCALAR_COLS:TOKENS])
+            if scalar_cols < TOKENS:
+                gpsimd_regroup(gg[:, scalar_cols:TOKENS, :], planes[s][:, :, scalar_cols:TOKENS])
             nc.scalar.copy(
-                out=interleaved(gg[:, 0:SCALAR_COLS, :]), in_=side_by_side(planes[s][:, :, 0:SCALAR_COLS])
+                out=interleaved(gg[:, 0:scalar_cols, :]), in_=side_by_side(planes[s][:, :, 0:scalar_cols])
             )
             grouped[s] = gg
 
@@ -271,11 +273,15 @@ def tile_hydraencoderlayer_pb_kernel(tc, x, wq, kv, wo, out):
                 stop=(c == CHUNKS - 1),
             )
 
-        def add_x_and_store(b, m):
+        def add_x_and_store(b, m, spare_vector):
+            x_tile = x_sb[:, b * TOKEN_TILES + m, :]
             result = store_pool.tile([P, D_MODEL], F32)
-            nc.vector.tensor_tensor(
-                out=result[:], in0=acc[m][:], in1=x_sb[:, b * TOKEN_TILES + m, :], op=ADD
-            )
+            if spare_vector:
+                product = store_pool.tile([P, D_MODEL], F32)
+                nc.scalar.copy(out=product[:], in_=acc[m][:])
+                nc.gpsimd.tensor_tensor(out=result[:], in0=product[:], in1=x_tile, op=ADD)
+            else:
+                nc.vector.tensor_tensor(out=result[:], in0=acc[m][:], in1=x_tile, op=ADD)
             nc.sync.dma_start(out=out[b, m * P : (m + 1) * P, :], in_=result[:])
 
         x_banks = {0: transpose_x(0, psum_val, "val")}
@@ -303,6 +309,7 @@ def tile_hydraencoderlayer_pb_kernel(tc, x, wq, kv, wo, out):
 
         for k in range(STEPS + OUT_LAG):
             s, t = divmod(k, PACK)
+            scalar_is_free = SQUARES_DONE <= k < STEPS
             late_x = s + 2 if s + 2 < BATCH else None
             if late_x is not None and t == 0:
                 x_banks[late_x] = transpose_x(late_x, psum_out, "out")
@@ -316,7 +323,7 @@ def tile_hydraencoderlayer_pb_kernel(tc, x, wq, kv, wo, out):
                 m, c = divmod(rest, CHUNKS)
                 out_pass(b, m, c)
                 if c == CHUNKS - 1:
-                    add_x_and_store(b, m)
+                    add_x_and_store(b, m, spare_vector=scalar_is_free)
             for b in range(1, BATCH):
                 last_norm_step = PACK * (TOKEN_TILES * (b + 1) - 1 - NORM_LEAD) + PACK - 1
                 if k == last_norm_step + NORMS_AFTER:
@@ -327,7 +334,7 @@ def tile_hydraencoderlayer_pb_kernel(tc, x, wq, kv, wo, out):
                 late_xg = gather_x(x_banks[late_x], nc.vector.tensor_copy)
             if t == PACK - 1:
                 if s < GROUPS:
-                    regroup_g(s)
+                    regroup_g(s, TOKENS if scalar_is_free else SCALAR_COLS)
                 if 1 <= s <= GROUPS:
                     quantise_g(s - 1)
                 if late_x is not None:

@@ -28,7 +28,8 @@ NORM_LEAD = TOKEN_TILES + 1
 OUT_LAG = STEPS // BATCH + PACK + 1
 SCALAR_COLS = TOKENS // 4
 NORMS_AFTER = 1
-SPREAD_AFTER = 3
+RECIPROCAL_AFTER = 2
+SPREAD_AFTER = 4
 SQUARES_DONE = PACK * (ALL_TILES - NORM_LEAD)
 
 FLOPS = 2 * BATCH * TOKENS * D_MODEL * D_INNER * 2
@@ -181,6 +182,7 @@ def tile_hydraencoderlayer_pb_kernel(tc, x, wq, kv, wo, out):
             )
 
         norms = {}
+        inv_cols = {}
         inv_norm = {}
 
         def floored_norms(b):
@@ -193,9 +195,13 @@ def tile_hydraencoderlayer_pb_kernel(tc, x, wq, kv, wo, out):
             nc.scalar.activation(out=norm[:], in_=excess[:], func=ACT.Sqrt, bias=EPS * EPS)
             norms[b] = norm
 
-        def spread_inverse_norms(b):
+        def invert_norms(b):
             rn = small.tile([P, TOKEN_TILES], F32)
             nc.vector.reciprocal(out=rn[:], in_=norms[b][:])
+            inv_cols[b] = rn
+
+        def spread_inverse_norms(b):
+            rn = inv_cols[b]
             spread = psum_norm.tile([P, TOKENS], F32, tag="norm")
             for m in range(TOKEN_TILES):
                 nc.tensor.transpose(
@@ -303,10 +309,15 @@ def tile_hydraencoderlayer_pb_kernel(tc, x, wq, kv, wo, out):
         prepare_wo(0)
         prepare_wo(1)
         floored_norms(0)
+        for tile in range(TOKEN_TILES, NORM_LEAD):
+            for c in range(CHUNKS):
+                norm_pass(tile, c)
         prepare_wo(2)
+        invert_norms(0)
         spread_inverse_norms(0)
         prepare_wo(3)
 
+        waiting_tile = None
         for k in range(STEPS + OUT_LAG):
             s, t = divmod(k, PACK)
             scalar_is_free = SQUARES_DONE <= k < STEPS
@@ -315,24 +326,30 @@ def tile_hydraencoderlayer_pb_kernel(tc, x, wq, kv, wo, out):
                 x_banks[late_x] = transpose_x(late_x, psum_out, "out")
             if s < GROUPS:
                 value_pass(s, t)
-                first_tile = TOKEN_TILES if s == 0 else s + NORM_LEAD
-                for tile in range(first_tile, min(s + NORM_LEAD + 1, ALL_TILES)):
-                    norm_pass(tile, t)
+                if s + NORM_LEAD < ALL_TILES:
+                    norm_pass(s + NORM_LEAD, t)
             if k >= OUT_LAG:
                 b, rest = divmod(k - OUT_LAG, TOKEN_TILES * CHUNKS)
                 m, c = divmod(rest, CHUNKS)
                 out_pass(b, m, c)
-                if c == CHUNKS - 1:
-                    add_x_and_store(b, m, spare_vector=scalar_is_free)
+                if c == CHUNKS - 1 and scalar_is_free:
+                    waiting_tile = (b, m)
+                elif c == CHUNKS - 1:
+                    add_x_and_store(b, m, spare_vector=False)
             for b in range(1, BATCH):
                 last_norm_step = PACK * (TOKEN_TILES * (b + 1) - 1 - NORM_LEAD) + PACK - 1
                 if k == last_norm_step + NORMS_AFTER:
                     floored_norms(b)
+                if k == last_norm_step + RECIPROCAL_AFTER:
+                    invert_norms(b)
                 if k == last_norm_step + SPREAD_AFTER:
                     spread_inverse_norms(b)
             if late_x is not None and t == PACK - 2:
                 late_xg = gather_x(x_banks[late_x], nc.vector.tensor_copy)
             if t == PACK - 1:
+                if waiting_tile is not None:
+                    add_x_and_store(waiting_tile[0], waiting_tile[1], spare_vector=True)
+                    waiting_tile = None
                 if s < GROUPS:
                     regroup_g(s, TOKENS if scalar_is_free else SCALAR_COLS)
                 if 1 <= s <= GROUPS:

@@ -30,6 +30,7 @@ SCALAR_COLS = TOKENS // 4
 NORMS_AFTER = 1
 RECIPROCAL_AFTER = 2
 SPREAD_AFTER = 4
+WQ1_SCALAR = 256
 SQUARES_DONE = PACK * (ALL_TILES - NORM_LEAD)
 
 FLOPS = 2 * BATCH * TOKENS * D_MODEL * D_INNER * 2
@@ -48,7 +49,7 @@ def tile_hydraencoderlayer_pb_kernel(tc, x, wq, kv, wo, out):
     with ExitStack() as ctx:
         keep = ctx.enter_context(tc.tile_pool(name="keep", bufs=1))
         raw_pool = ctx.enter_context(tc.tile_pool(name="raw", bufs=2 * CHUNKS))
-        stage = ctx.enter_context(tc.tile_pool(name="stage", bufs=3))
+        stage = ctx.enter_context(tc.tile_pool(name="stage", bufs=4))
         code_pool = ctx.enter_context(tc.tile_pool(name="g_codes", bufs=2 * CHUNKS))
         junk_pool = ctx.enter_context(tc.tile_pool(name="junk", bufs=4))
         small = ctx.enter_context(tc.tile_pool(name="small", bufs=2))
@@ -150,9 +151,15 @@ def tile_hydraencoderlayer_pb_kernel(tc, x, wq, kv, wo, out):
                 op1=ADD,
             )
 
-        def regroup_weight(raw):
+        def regroup_weight(raw, scalar_cols=0):
             wg = stage.tile([P, K_PASS, PACK], BF16, tag="wg", align_bytes=64)
-            nc.vector.tensor_copy(out=interleaved(wg[:]), in_=side_by_side(raw[:]))
+            if scalar_cols:
+                nc.scalar.copy(
+                    out=interleaved(wg[:, 0:scalar_cols, :]), in_=side_by_side(raw[:, :, 0:scalar_cols])
+                )
+            nc.vector.tensor_copy(
+                out=interleaved(wg[:, scalar_cols:K_PASS, :]), in_=side_by_side(raw[:, :, scalar_cols:K_PASS])
+            )
             return wg
 
         def quantise_wq(c, wg):
@@ -298,14 +305,22 @@ def tile_hydraencoderlayer_pb_kernel(tc, x, wq, kv, wo, out):
         kv_ps = psum_norm.tile([P, P], BF16, tag="norm")
         nc.tensor.transpose(kv_ps[:], kv_rows[:], ident_bf16[:])
         nc.vector.tensor_copy(out=kv_cols[:], in_=kv_ps[:, 0 : BATCH * FEATURE_TILES])
+        wg = regroup_weight(wq_raw[1], WQ1_SCALAR)
         for c in range(CHUNKS):
             for tile in range(TOKEN_TILES):
                 norm_pass(tile, c)
-            if c + 1 < CHUNKS:
+            if c == 0:
+                quantise_wq(1, wg)
+            elif c + 1 < CHUNKS:
                 quantise_wq(c + 1, regroup_weight(wq_raw[c + 1]))
             if c == 1:
                 x_banks[1] = transpose_x(1, psum_val, "val")
         quantise(gather_x(x_banks[1], nc.vector.tensor_copy), x_codes[:, 1, :], x_scales[:, 1, :])
+        late_xg = {}
+        x_banks[2] = transpose_x(2, psum_out, "out")
+        x_banks[3] = transpose_x(3, psum_val, "val")
+        for b in (2, 3):
+            late_xg[b] = gather_x(x_banks[b], nc.scalar.copy)
         prepare_wo(0)
         prepare_wo(1)
         floored_norms(0)
@@ -322,8 +337,6 @@ def tile_hydraencoderlayer_pb_kernel(tc, x, wq, kv, wo, out):
             s, t = divmod(k, PACK)
             scalar_is_free = SQUARES_DONE <= k < STEPS
             late_x = s + 2 if s + 2 < BATCH else None
-            if late_x is not None and t == 0:
-                x_banks[late_x] = transpose_x(late_x, psum_out, "out")
             if s < GROUPS:
                 value_pass(s, t)
                 if s + NORM_LEAD < ALL_TILES:
@@ -344,8 +357,6 @@ def tile_hydraencoderlayer_pb_kernel(tc, x, wq, kv, wo, out):
                     invert_norms(b)
                 if k == last_norm_step + SPREAD_AFTER:
                     spread_inverse_norms(b)
-            if late_x is not None and t == PACK - 2:
-                late_xg = gather_x(x_banks[late_x], nc.vector.tensor_copy)
             if t == PACK - 1:
                 if waiting_tile is not None:
                     add_x_and_store(waiting_tile[0], waiting_tile[1], spare_vector=True)
@@ -355,4 +366,4 @@ def tile_hydraencoderlayer_pb_kernel(tc, x, wq, kv, wo, out):
                 if 1 <= s <= GROUPS:
                     quantise_g(s - 1)
                 if late_x is not None:
-                    quantise(late_xg, x_codes[:, late_x, :], x_scales[:, late_x, :])
+                    quantise(late_xg[late_x], x_codes[:, late_x, :], x_scales[:, late_x, :])

@@ -31,6 +31,14 @@ NORMS_AFTER = 1
 RECIPROCAL_AFTER = 2
 SPREAD_AFTER = 4
 WQ1_SCALAR = 256
+EARLY_CHUNKS = 0
+LAST_FROM = ()
+LATE_SCALAR = 512
+EARLY_SCALAR = 128
+EARLY_GROUPS = 5
+SCALAR_END = 256
+LATE_NORM = (2, 3, 4)
+VECTOR_END = 256
 SQUARES_DONE = PACK * (ALL_TILES - NORM_LEAD)
 
 FLOPS = 2 * BATCH * TOKENS * D_MODEL * D_INNER * 2
@@ -67,6 +75,7 @@ def tile_hydraencoderlayer_pb_kernel(tc, x, wq, kv, wo, out):
         nc.vector.memset(warm[:], 1.0)
         nc.scalar.activation(out=warm[:], in_=warm[:], func=ACT.Sqrt)
 
+        out_view = out.rearrange("b (p m) d -> b m p d", m=TOKEN_TILES)
         x_sb = keep.tile([P, ALL_TILES, D_MODEL], BF16)
         x_codes = keep.tile([P, BATCH, TOKENS], U32, align_bytes=64)
         x_scales = keep.tile([P, BATCH, TOKENS], U8, align_bytes=64)
@@ -81,7 +90,7 @@ def tile_hydraencoderlayer_pb_kernel(tc, x, wq, kv, wo, out):
         def load_x(b):
             nc.sync.dma_start(
                 out=x_sb[:, b * TOKEN_TILES : (b + 1) * TOKEN_TILES, :],
-                in_=x[b].rearrange("(m p) d -> p m d", p=P),
+                in_=x[b].rearrange("(p m) d -> p m d", p=P),
             )
 
         load_x(0)
@@ -103,8 +112,8 @@ def tile_hydraencoderlayer_pb_kernel(tc, x, wq, kv, wo, out):
             raw = raw_pool.tile([P, PACK, D_MODEL], BF16, tag="raw")
             nc.sync.dma_start(out=raw[:], in_=wo_view[c])
             wo_raw.append(raw)
-        load_x(2)
-        load_x(3)
+            if c + 2 < BATCH:
+                load_x(c + 2)
         nc.vector.memset(kv_rows[:], 0.0)
         nc.scalar.dma_start(
             out=kv_rows[0 : BATCH * FEATURE_TILES, :], in_=kv.rearrange("b o (j p) -> (b o j) p", p=P)
@@ -249,14 +258,22 @@ def tile_hydraencoderlayer_pb_kernel(tc, x, wq, kv, wo, out):
 
         grouped = {}
 
-        def regroup_g(s, scalar_cols):
+        def regroup_g(s, scalar_cols, vector_cols=0):
             gg = stage.tile([P, TOKENS, PACK], BF16, tag="gg", align_bytes=64)
-            if scalar_cols < TOKENS:
-                gpsimd_regroup(gg[:, scalar_cols:TOKENS, :], planes[s][:, :, scalar_cols:TOKENS])
-            nc.scalar.copy(
-                out=interleaved(gg[:, 0:scalar_cols, :]), in_=side_by_side(planes[s][:, :, 0:scalar_cols])
-            )
             grouped[s] = gg
+            gpsimd_end = TOKENS - vector_cols
+            if scalar_cols < gpsimd_end:
+                gpsimd_regroup(gg[:, scalar_cols:gpsimd_end, :], planes[s][:, :, scalar_cols:gpsimd_end])
+            if vector_cols:
+                nc.vector.tensor_copy(
+                    out=interleaved(gg[:, gpsimd_end:TOKENS, :]), in_=side_by_side(planes[s][:, :, gpsimd_end:TOKENS])
+                )
+
+        def regroup_g_scalar(s, scalar_cols):
+            nc.scalar.copy(
+                out=interleaved(grouped[s][:, 0:scalar_cols, :]), in_=side_by_side(planes[s][:, :, 0:scalar_cols])
+            )
+
 
         g_codes = {}
         g_scales = {}
@@ -270,14 +287,14 @@ def tile_hydraencoderlayer_pb_kernel(tc, x, wq, kv, wo, out):
 
         acc = {}
 
-        def out_pass(b, m, c):
+        def out_pass(b, m, c, pool, tag):
             s = b * CHUNKS + c
             tokens = slice(m * P, (m + 1) * P)
             if c == 0:
-                bank = psum_out.tile([P, D_MODEL], F32, tag="out")
-                acc[m] = bank
+                bank = pool.tile([P, D_MODEL], F32, tag=tag)
+                acc[b, m] = bank
             nc.tensor.matmul_mx(
-                out=acc[m][:],
+                out=acc[b, m][:],
                 lhsT=g_codes[s][:, tokens].bitcast(FP8X4),
                 lhsT_scale=g_scales[s][:, tokens],
                 rhs=wo_codes[:, c, :].bitcast(FP8X4),
@@ -291,11 +308,11 @@ def tile_hydraencoderlayer_pb_kernel(tc, x, wq, kv, wo, out):
             result = store_pool.tile([P, D_MODEL], F32)
             if spare_vector:
                 product = store_pool.tile([P, D_MODEL], F32)
-                nc.scalar.copy(out=product[:], in_=acc[m][:])
+                nc.scalar.copy(out=product[:], in_=acc[b, m][:])
                 nc.gpsimd.tensor_tensor(out=result[:], in0=product[:], in1=x_tile, op=ADD)
             else:
-                nc.vector.tensor_tensor(out=result[:], in0=acc[m][:], in1=x_tile, op=ADD)
-            nc.sync.dma_start(out=out[b, m * P : (m + 1) * P, :], in_=result[:])
+                nc.vector.tensor_tensor(out=result[:], in0=acc[b, m][:], in1=x_tile, op=ADD)
+            nc.sync.dma_start(out=out_view[b, m], in_=result[:])
 
         x_banks = {0: transpose_x(0, psum_val, "val")}
         xg = gather_x(x_banks[0], nc.scalar.copy)
@@ -332,21 +349,34 @@ def tile_hydraencoderlayer_pb_kernel(tc, x, wq, kv, wo, out):
         spread_inverse_norms(0)
         prepare_wo(3)
 
-        waiting_tile = None
-        for k in range(STEPS + OUT_LAG):
+        plan = {}
+        for b in range(BATCH - 1):
+            first = b * STEPS // BATCH + OUT_LAG
+            for m in range(TOKEN_TILES):
+                for c in range(CHUNKS):
+                    n = m * CHUNKS + c
+                    plan.setdefault(first + (n * 2 // 3 if b == 2 else n), []).append((b, m, c))
+        for c in range(EARLY_CHUNKS):
+            for m in range(TOKEN_TILES):
+                plan.setdefault(LAST_FROM[c] + m // 2, []).append((BATCH - 1, m, c))
+        waiting = []
+        late_banks = 0
+        for k in range(STEPS):
             s, t = divmod(k, PACK)
-            scalar_is_free = SQUARES_DONE <= k < STEPS
+            scalar_is_free = SQUARES_DONE <= k
             late_x = s + 2 if s + 2 < BATCH else None
-            if s < GROUPS:
-                value_pass(s, t)
-                if s + NORM_LEAD < ALL_TILES:
-                    norm_pass(s + NORM_LEAD, t)
-            if k >= OUT_LAG:
-                b, rest = divmod(k - OUT_LAG, TOKEN_TILES * CHUNKS)
-                m, c = divmod(rest, CHUNKS)
-                out_pass(b, m, c)
+            value_pass(s, t)
+            if s + NORM_LEAD < ALL_TILES:
+                norm_pass(s + NORM_LEAD, t)
+            for b, m, c in plan.get(k, ()):
+                if c == 0 and k >= SQUARES_DONE:
+                    late_banks += 1
+                if k >= SQUARES_DONE and late_banks % 5 in LATE_NORM:
+                    out_pass(b, m, c, psum_norm, "norm")
+                else:
+                    out_pass(b, m, c, psum_out, "out")
                 if c == CHUNKS - 1 and scalar_is_free:
-                    waiting_tile = (b, m)
+                    waiting.append((b, m))
                 elif c == CHUNKS - 1:
                     add_x_and_store(b, m, spare_vector=False)
             for b in range(1, BATCH):
@@ -358,12 +388,34 @@ def tile_hydraencoderlayer_pb_kernel(tc, x, wq, kv, wo, out):
                 if k == last_norm_step + SPREAD_AFTER:
                     spread_inverse_norms(b)
             if t == PACK - 1:
-                if waiting_tile is not None:
-                    add_x_and_store(waiting_tile[0], waiting_tile[1], spare_vector=True)
-                    waiting_tile = None
-                if s < GROUPS:
-                    regroup_g(s, TOKENS if scalar_is_free else SCALAR_COLS)
-                if 1 <= s <= GROUPS:
+                if s == GROUPS - 1:
+                    scalar_cols, vector_cols = SCALAR_END, VECTOR_END
+                    for b, m in waiting:
+                        add_x_and_store(b, m, spare_vector=False)
+                    waiting = []
+                    quantise_g(s - 1)
+                else:
+                    scalar_cols, vector_cols = LATE_SCALAR if scalar_is_free else (EARLY_SCALAR if s < EARLY_GROUPS else SCALAR_COLS), 0
+                regroup_g(s, scalar_cols, vector_cols)
+                for n, (b, m) in enumerate(waiting):
+                    add_x_and_store(b, m, spare_vector=n == 0)
+                waiting = []
+                if scalar_cols:
+                    regroup_g_scalar(s, scalar_cols)
+                if 1 <= s < GROUPS - 1:
                     quantise_g(s - 1)
                 if late_x is not None:
                     quantise(late_xg[late_x], x_codes[:, late_x, :], x_scales[:, late_x, :])
+        b = BATCH - 1
+        for c in range(EARLY_CHUNKS, CHUNKS - 1):
+            for m in range(TOKEN_TILES):
+                if c == 0:
+                    late_banks += 1
+                if late_banks % 5 in LATE_NORM:
+                    out_pass(b, m, c, psum_norm, "norm")
+                else:
+                    out_pass(b, m, c, psum_out, "out")
+        quantise_g(GROUPS - 1)
+        for m in range(TOKEN_TILES):
+            out_pass(b, m, CHUNKS - 1, psum_out, "out")
+            add_x_and_store(b, m, spare_vector=False)

@@ -35,6 +35,7 @@ EARLY_CHUNKS = 0
 LAST_FROM = ()
 LATE_SCALAR = 512
 EARLY_SCALAR = 128
+EXTRA_NORMS = (3,)
 EARLY_GROUPS = 5
 SCALAR_END = 256
 LATE_NORM = (2, 3, 4)
@@ -73,7 +74,7 @@ def tile_hydraencoderlayer_pb_kernel(tc, x, wq, kv, wo, out):
         make_identity(nc, ident_bf16[:])
         warm = keep.tile([P, 1], F32)
         nc.vector.memset(warm[:], 1.0)
-        nc.scalar.activation(out=warm[:], in_=warm[:], func=ACT.Sqrt)
+        nc.scalar.activation(out=warm[:], in_=warm[:], func=ACT.Abs_reciprocal_sqrt)
 
         out_view = out.rearrange("b (p m) d -> b m p d", m=TOKEN_TILES)
         x_sb = keep.tile([P, ALL_TILES, D_MODEL], BF16)
@@ -197,7 +198,6 @@ def tile_hydraencoderlayer_pb_kernel(tc, x, wq, kv, wo, out):
                 out=squares[:], in_=a_tok[:], func=ACT.Square, accum_out=sumsq[:, tile, c : c + 1]
             )
 
-        norms = {}
         inv_cols = {}
         inv_norm = {}
 
@@ -207,13 +207,8 @@ def tile_hydraencoderlayer_pb_kernel(tc, x, wq, kv, wo, out):
             nc.vector.tensor_reduce(out=n2[:], in_=sumsq[:, tiles, :], axis=mybir.AxisListType.X, op=ADD)
             excess = small.tile([P, TOKEN_TILES], F32)
             nc.scalar.activation(out=excess[:], in_=n2[:], func=ACT.Relu, bias=-EPS * EPS)
-            norm = small.tile([P, TOKEN_TILES], F32)
-            nc.scalar.activation(out=norm[:], in_=excess[:], func=ACT.Sqrt, bias=EPS * EPS)
-            norms[b] = norm
-
-        def invert_norms(b):
             rn = small.tile([P, TOKEN_TILES], F32)
-            nc.vector.reciprocal(out=rn[:], in_=norms[b][:])
+            nc.scalar.activation(out=rn[:], in_=excess[:], func=ACT.Abs_reciprocal_sqrt, bias=EPS * EPS)
             inv_cols[b] = rn
 
         def spread_inverse_norms(b):
@@ -345,7 +340,6 @@ def tile_hydraencoderlayer_pb_kernel(tc, x, wq, kv, wo, out):
             for c in range(CHUNKS):
                 norm_pass(tile, c)
         prepare_wo(2)
-        invert_norms(0)
         spread_inverse_norms(0)
         prepare_wo(3)
 
@@ -359,6 +353,12 @@ def tile_hydraencoderlayer_pb_kernel(tc, x, wq, kv, wo, out):
         for c in range(EARLY_CHUNKS):
             for m in range(TOKEN_TILES):
                 plan.setdefault(LAST_FROM[c] + m // 2, []).append((BATCH - 1, m, c))
+        norm_plan = []
+        done = NORM_LEAD * CHUNKS
+        for k in range(STEPS):
+            n = 2 if k in EXTRA_NORMS else 1
+            norm_plan.append(range(done, min(done + n, ALL_TILES * CHUNKS)))
+            done = min(done + n, ALL_TILES * CHUNKS)
         waiting = []
         late_banks = 0
         for k in range(STEPS):
@@ -366,8 +366,8 @@ def tile_hydraencoderlayer_pb_kernel(tc, x, wq, kv, wo, out):
             scalar_is_free = SQUARES_DONE <= k
             late_x = s + 2 if s + 2 < BATCH else None
             value_pass(s, t)
-            if s + NORM_LEAD < ALL_TILES:
-                norm_pass(s + NORM_LEAD, t)
+            for n in norm_plan[k]:
+                norm_pass(*divmod(n, CHUNKS))
             for b, m, c in plan.get(k, ()):
                 if c == 0 and k >= SQUARES_DONE:
                     late_banks += 1
@@ -380,11 +380,11 @@ def tile_hydraencoderlayer_pb_kernel(tc, x, wq, kv, wo, out):
                 elif c == CHUNKS - 1:
                     add_x_and_store(b, m, spare_vector=False)
             for b in range(1, BATCH):
-                last_norm_step = PACK * (TOKEN_TILES * (b + 1) - 1 - NORM_LEAD) + PACK - 1
+                last_norm_step = [
+                    q for q in range(STEPS) if CHUNKS * TOKEN_TILES * (b + 1) - 1 in norm_plan[q]
+                ][0]
                 if k == last_norm_step + NORMS_AFTER:
                     floored_norms(b)
-                if k == last_norm_step + RECIPROCAL_AFTER:
-                    invert_norms(b)
                 if k == last_norm_step + SPREAD_AFTER:
                     spread_inverse_norms(b)
             if t == PACK - 1:

@@ -153,8 +153,8 @@ def tile_hydraencoderlayer_pb_kernel(tc, x, wq, kv, wo, out):
 
         def gpsimd_regroup(grouped_cols, plane_cols):
             nc.gpsimd.tensor_scalar(
-                out=grouped_cols,
-                in0=plane_cols.rearrange("p t w -> p w t"),
+                out=interleaved(grouped_cols),
+                in0=side_by_side(plane_cols),
                 scalar1=1.0,
                 scalar2=0.0,
                 op0=MULT,

from contextlib import ExitStack

import concourse.mybir as mybir
from concourse.masks import make_identity

F32 = mybir.dt.float32
BF16 = mybir.dt.bfloat16
U32 = mybir.dt.uint32
U8 = mybir.dt.uint8
FP8X4 = mybir.dt.float8_e4m3fn_x4
MULT = mybir.AluOpType.mult
ADD = mybir.AluOpType.add
ACT = mybir.ActivationFunctionType

P = 128
PACK = 4
K_PASS = P * PACK
BATCH, TOKENS, D_MODEL, D_INNER = 4, 512, 512, 2048
TOKEN_TILES = TOKENS // P
ALL_TILES = BATCH * TOKEN_TILES
CHUNKS = D_INNER // K_PASS
FEATURE_TILES = D_INNER // P
GROUPS = BATCH * CHUNKS
STEPS = GROUPS * PACK
EPS = 1e-12

NORM_LEAD = TOKEN_TILES + 1
OUT_LAG = STEPS // BATCH + PACK + 1
SCALAR_COLS = TOKENS // 4
NORMS_AFTER = 1
RECIPROCAL_AFTER = 2
SPREAD_AFTER = 4
WQ1_SCALAR = 256
EARLY_CHUNKS = 0
LAST_FROM = ()
LATE_SCALAR = 512
EARLY_SCALAR = 128
EXTRA_NORMS = (3,)
EARLY_GROUPS = 5
SCALAR_END = 256
LATE_NORM = (2, 3, 4)
VECTOR_END = 256
SQUARES_DONE = PACK * (ALL_TILES - NORM_LEAD)

FLOPS = 2 * BATCH * TOKENS * D_MODEL * D_INNER * 2


def side_by_side(planes):
    return planes.rearrange("p t (c i) -> p c t i", i=4)


def interleaved(grouped):
    return grouped.rearrange("p (c i) t -> p c t i", i=4)


def tile_hydraencoderlayer_pb_kernel(tc, x, wq, kv, wo, out):
    nc = tc.nc
    with ExitStack() as ctx:
        keep = ctx.enter_context(tc.tile_pool(name="keep", bufs=1))
        raw_pool = ctx.enter_context(tc.tile_pool(name="raw", bufs=2 * CHUNKS))
        stage = ctx.enter_context(tc.tile_pool(name="stage", bufs=4))
        code_pool = ctx.enter_context(tc.tile_pool(name="g_codes", bufs=2 * CHUNKS))
        junk_pool = ctx.enter_context(tc.tile_pool(name="junk", bufs=4))
        small = ctx.enter_context(tc.tile_pool(name="small", bufs=2))
        store_pool = ctx.enter_context(tc.tile_pool(name="store", bufs=4))
        psum_val = ctx.enter_context(tc.psum_pool(name="psum_val", bufs=3))
        psum_norm = ctx.enter_context(tc.psum_pool(name="psum_norm", bufs=3))
        psum_out = ctx.enter_context(tc.psum_pool(name="psum_out", bufs=2))
        ctx.enter_context(tc.manual_schedule())

        ident_f32 = keep.tile([P, P], F32)
        make_identity(nc, ident_f32[:])
        ident_bf16 = keep.tile([P, P], BF16)
        make_identity(nc, ident_bf16[:])
        warm = keep.tile([P, 1], F32)
        nc.vector.memset(warm[:], 1.0)
        nc.scalar.activation(out=warm[:], in_=warm[:], func=ACT.Abs_reciprocal_sqrt)

        out_view = out.rearrange("b (p m) d -> b m p d", m=TOKEN_TILES)
        x_sb = keep.tile([P, ALL_TILES, D_MODEL], BF16)
        x_codes = keep.tile([P, BATCH, TOKENS], U32, align_bytes=64)
        x_scales = keep.tile([P, BATCH, TOKENS], U8, align_bytes=64)
        wq_codes = keep.tile([P, D_INNER], U32, align_bytes=64)
        wq_scales = keep.tile([P, D_INNER], U8, align_bytes=64)
        wo_codes = keep.tile([P, CHUNKS, D_MODEL], U32, align_bytes=64)
        wo_scales = keep.tile([P, CHUNKS, D_MODEL], U8, align_bytes=64)
        kv_rows = keep.tile([P, P], BF16)
        kv_cols = keep.tile([P, BATCH * FEATURE_TILES], F32)
        sumsq = keep.tile([P, ALL_TILES, CHUNKS], F32)

        def load_x(b):
            nc.sync.dma_start(
                out=x_sb[:, b * TOKEN_TILES : (b + 1) * TOKEN_TILES, :],
                in_=x[b].rearrange("(p m) d -> p m d", p=P),
            )

        load_x(0)
        wq_raw = []
        for c in range(CHUNKS):
            raw = raw_pool.tile([P, PACK, K_PASS], BF16, tag="raw")
            for u in range(2):
                nc.sync.dma_start(
                    out=raw[:, 2 * u : 2 * u + 2, :],
                    in_=wq[2 * P * u : 2 * P * (u + 1), c * K_PASS : (c + 1) * K_PASS].rearrange(
                        "(p e) c -> p e c", e=2
                    ),
                )
            wq_raw.append(raw)
        load_x(1)
        wo_raw = []
        wo_view = wo.rearrange("(c t p) n -> c p t n", t=PACK, p=P)
        for c in range(CHUNKS):
            raw = raw_pool.tile([P, PACK, D_MODEL], BF16, tag="raw")
            nc.sync.dma_start(out=raw[:], in_=wo_view[c])
            wo_raw.append(raw)
            if c + 2 < BATCH:
                load_x(c + 2)
        nc.vector.memset(kv_rows[:], 0.0)
        nc.scalar.dma_start(
            out=kv_rows[0 : BATCH * FEATURE_TILES, :], in_=kv.rearrange("b o (j p) -> (b o j) p", p=P)
        )

        x_words = x_sb[:].bitcast(F32)

        def transpose_x(b, psum_pool, tag):
            banks = []
            for h in range(2):
                xt = psum_pool.tile([P, 2, 2, P], F32, tag=tag)
                for m in range(2):
                    for u in range(2):
                        nc.tensor.transpose(
                            xt[:, m, u, :],
                            x_words[:, b * TOKEN_TILES + 2 * h + m, u * P : (u + 1) * P],
                            ident_f32[:],
                        )
                banks.append(xt)
            return banks

        def gather_x(banks, copy):
            xg = stage.tile([P, TOKENS, PACK], BF16, tag="xg", align_bytes=64)
            xg_words = xg[:].bitcast(F32)
            for h in range(2):
                copy(
                    out=xg_words[:, 2 * P * h : 2 * P * (h + 1), :].rearrange("p (m r) u -> p m r u", m=2),
                    in_=banks[h][:].rearrange("p m u r -> p m r u"),
                )
            return xg

        def quantise(grouped, codes, scales):
            nc.vector.quantize_mx(
                out=codes.bitcast(FP8X4), scales=scales, in_=grouped[:].rearrange("p w j -> p (w j)")
            )

        def gpsimd_regroup(grouped_cols, plane_cols):
            nc.gpsimd.tensor_scalar(
                out=interleaved(grouped_cols),
                in0=side_by_side(plane_cols),
                scalar1=1.0,
                scalar2=0.0,
                op0=MULT,
                op1=ADD,
            )

        def regroup_weight(raw, scalar_cols=0):
            wg = stage.tile([P, K_PASS, PACK], BF16, tag="wg", align_bytes=64)
            if scalar_cols:
                nc.scalar.copy(
                    out=interleaved(wg[:, 0:scalar_cols, :]), in_=side_by_side(raw[:, :, 0:scalar_cols])
                )
            nc.vector.tensor_copy(
                out=interleaved(wg[:, scalar_cols:K_PASS, :]), in_=side_by_side(raw[:, :, scalar_cols:K_PASS])
            )
            return wg

        def quantise_wq(c, wg):
            cols = slice(c * K_PASS, (c + 1) * K_PASS)
            quantise(wg, wq_codes[:, cols], wq_scales[:, cols])

        def prepare_wo(c):
            quantise(regroup_weight(wo_raw[c]), wo_codes[:, c, :], wo_scales[:, c, :])

        def norm_pass(tile, c):
            b, m = divmod(tile, TOKEN_TILES)
            tokens = slice(m * P, (m + 1) * P)
            cols = slice(c * K_PASS, (c + 1) * K_PASS)
            a_tok = psum_norm.tile([P, K_PASS], F32, tag="norm")
            nc.tensor.matmul_mx(
                out=a_tok[:],
                lhsT=x_codes[:, b, tokens].bitcast(FP8X4),
                lhsT_scale=x_scales[:, b, tokens],
                rhs=wq_codes[:, cols].bitcast(FP8X4),
                rhs_scale=wq_scales[:, cols],
                start=True,
                stop=True,
            )
            squares = junk_pool.tile([P, K_PASS], BF16)
            nc.scalar.activation(
                out=squares[:], in_=a_tok[:], func=ACT.Square, accum_out=sumsq[:, tile, c : c + 1]
            )

        inv_cols = {}
        inv_norm = {}

        def floored_norms(b):
            tiles = slice(b * TOKEN_TILES, (b + 1) * TOKEN_TILES)
            n2 = small.tile([P, TOKEN_TILES], F32)
            nc.vector.tensor_reduce(out=n2[:], in_=sumsq[:, tiles, :], axis=mybir.AxisListType.X, op=ADD)
            excess = small.tile([P, TOKEN_TILES], F32)
            nc.scalar.activation(out=excess[:], in_=n2[:], func=ACT.Relu, bias=-EPS * EPS)
            rn = small.tile([P, TOKEN_TILES], F32)
            nc.scalar.activation(out=rn[:], in_=excess[:], func=ACT.Abs_reciprocal_sqrt, bias=EPS * EPS)
            inv_cols[b] = rn

        def spread_inverse_norms(b):
            rn = inv_cols[b]
            spread = psum_norm.tile([P, TOKENS], F32, tag="norm")
            for m in range(TOKEN_TILES):
                nc.tensor.transpose(
                    spread[:, m * P : (m + 1) * P], rn[:, m : m + 1].to_broadcast([P, P]), ident_f32[:]
                )
            rn_all = small.tile([P, TOKENS], F32)
            nc.scalar.copy(out=rn_all[:], in_=spread[:])
            inv_norm[b] = rn_all

        planes = {}

        def value_pass(s, t):
            b, c = divmod(s, CHUNKS)
            j = PACK * c + t
            feats = slice(j * P, (j + 1) * P)
            if t == 0:
                new_planes = stage.tile([P, PACK, TOKENS], BF16, tag="planes")
                planes[s] = new_planes
            a_feat = psum_val.tile([P, TOKENS], F32, tag="val")
            nc.tensor.matmul_mx(
                out=a_feat[:],
                lhsT=wq_codes[:, feats].bitcast(FP8X4),
                lhsT_scale=wq_scales[:, feats],
                rhs=x_codes[:, b, :].bitcast(FP8X4),
                rhs_scale=x_scales[:, b, :],
                start=True,
                stop=True,
            )
            col = b * FEATURE_TILES + j
            nc.vector.scalar_tensor_tensor(
                out=planes[s][:, t, :],
                in0=a_feat[:],
                scalar=kv_cols[:, col : col + 1],
                in1=inv_norm[b][:],
                op0=MULT,
                op1=MULT,
            )

        grouped = {}

        def regroup_g(s, scalar_cols, vector_cols=0):
            gg = stage.tile([P, TOKENS, PACK], BF16, tag="gg", align_bytes=64)
            grouped[s] = gg
            gpsimd_end = TOKENS - vector_cols
            if scalar_cols < gpsimd_end:
                gpsimd_regroup(gg[:, scalar_cols:gpsimd_end, :], planes[s][:, :, scalar_cols:gpsimd_end])
            if vector_cols:
                nc.vector.tensor_copy(
                    out=interleaved(gg[:, gpsimd_end:TOKENS, :]), in_=side_by_side(planes[s][:, :, gpsimd_end:TOKENS])
                )

        def regroup_g_scalar(s, scalar_cols):
            nc.scalar.copy(
                out=interleaved(grouped[s][:, 0:scalar_cols, :]), in_=side_by_side(planes[s][:, :, 0:scalar_cols])
            )


        g_codes = {}
        g_scales = {}

        def quantise_g(s):
            codes = code_pool.tile([P, TOKENS], U32, tag="codes", align_bytes=64)
            scales = code_pool.tile([P, TOKENS], U8, tag="scales", align_bytes=64)
            quantise(grouped[s], codes[:], scales[:])
            g_codes[s] = codes
            g_scales[s] = scales

        acc = {}

        def out_pass(b, m, c, pool, tag):
            s = b * CHUNKS + c
            tokens = slice(m * P, (m + 1) * P)
            if c == 0:
                bank = pool.tile([P, D_MODEL], F32, tag=tag)
                acc[b, m] = bank
            nc.tensor.matmul_mx(
                out=acc[b, m][:],
                lhsT=g_codes[s][:, tokens].bitcast(FP8X4),
                lhsT_scale=g_scales[s][:, tokens],
                rhs=wo_codes[:, c, :].bitcast(FP8X4),
                rhs_scale=wo_scales[:, c, :],
                start=(c == 0),
                stop=(c == CHUNKS - 1),
            )

        def add_x_and_store(b, m, spare_vector):
            x_tile = x_sb[:, b * TOKEN_TILES + m, :]
            result = store_pool.tile([P, D_MODEL], F32)
            if spare_vector:
                product = store_pool.tile([P, D_MODEL], F32)
                nc.scalar.copy(out=product[:], in_=acc[b, m][:])
                nc.gpsimd.tensor_tensor(out=result[:], in0=product[:], in1=x_tile, op=ADD)
            else:
                nc.vector.tensor_tensor(out=result[:], in0=acc[b, m][:], in1=x_tile, op=ADD)
            nc.sync.dma_start(out=out_view[b, m], in_=result[:])

        x_banks = {0: transpose_x(0, psum_val, "val")}
        xg = gather_x(x_banks[0], nc.scalar.copy)
        wg = regroup_weight(wq_raw[0])
        quantise(xg, x_codes[:, 0, :], x_scales[:, 0, :])
        quantise_wq(0, wg)
        kv_ps = psum_norm.tile([P, P], BF16, tag="norm")
        nc.tensor.transpose(kv_ps[:], kv_rows[:], ident_bf16[:])
        nc.vector.tensor_copy(out=kv_cols[:], in_=kv_ps[:, 0 : BATCH * FEATURE_TILES])
        wg = regroup_weight(wq_raw[1], WQ1_SCALAR)
        for c in range(CHUNKS):
            for tile in range(TOKEN_TILES):
                norm_pass(tile, c)
            if c == 0:
                quantise_wq(1, wg)
            elif c + 1 < CHUNKS:
                quantise_wq(c + 1, regroup_weight(wq_raw[c + 1]))
            if c == 1:
                x_banks[1] = transpose_x(1, psum_val, "val")
        quantise(gather_x(x_banks[1], nc.vector.tensor_copy), x_codes[:, 1, :], x_scales[:, 1, :])
        late_xg = {}
        x_banks[2] = transpose_x(2, psum_out, "out")
        x_banks[3] = transpose_x(3, psum_val, "val")
        for b in (2, 3):
            late_xg[b] = gather_x(x_banks[b], nc.scalar.copy)
        prepare_wo(0)
        prepare_wo(1)
        floored_norms(0)
        for tile in range(TOKEN_TILES, NORM_LEAD):
            for c in range(CHUNKS):
                norm_pass(tile, c)
        prepare_wo(2)
        spread_inverse_norms(0)
        prepare_wo(3)

        plan = {}
        for b in range(BATCH - 1):
            first = b * STEPS // BATCH + OUT_LAG
            for m in range(TOKEN_TILES):
                for c in range(CHUNKS):
                    n = m * CHUNKS + c
                    plan.setdefault(first + (n * 2 // 3 if b == 2 else n), []).append((b, m, c))
        for c in range(EARLY_CHUNKS):
            for m in range(TOKEN_TILES):
                plan.setdefault(LAST_FROM[c] + m // 2, []).append((BATCH - 1, m, c))
        norm_plan = []
        done = NORM_LEAD * CHUNKS
        for k in range(STEPS):
            n = 2 if k in EXTRA_NORMS else 1
            norm_plan.append(range(done, min(done + n, ALL_TILES * CHUNKS)))
            done = min(done + n, ALL_TILES * CHUNKS)
        waiting = []
        late_banks = 0
        for k in range(STEPS):
            s, t = divmod(k, PACK)
            scalar_is_free = SQUARES_DONE <= k
            late_x = s + 2 if s + 2 < BATCH else None
            value_pass(s, t)
            for n in norm_plan[k]:
                norm_pass(*divmod(n, CHUNKS))
            for b, m, c in plan.get(k, ()):
                if c == 0 and k >= SQUARES_DONE:
                    late_banks += 1
                if k >= SQUARES_DONE and late_banks % 5 in LATE_NORM:
                    out_pass(b, m, c, psum_norm, "norm")
                else:
                    out_pass(b, m, c, psum_out, "out")
                if c == CHUNKS - 1 and scalar_is_free:
                    waiting.append((b, m))
                elif c == CHUNKS - 1:
                    add_x_and_store(b, m, spare_vector=False)
            for b in range(1, BATCH):
                last_norm_step = [
                    q for q in range(STEPS) if CHUNKS * TOKEN_TILES * (b + 1) - 1 in norm_plan[q]
                ][0]
                if k == last_norm_step + NORMS_AFTER:
                    floored_norms(b)
                if k == last_norm_step + SPREAD_AFTER:
                    spread_inverse_norms(b)
            if t == PACK - 1:
                if s == GROUPS - 1:
                    scalar_cols, vector_cols = SCALAR_END, VECTOR_END
                    for b, m in waiting:
                        add_x_and_store(b, m, spare_vector=False)
                    waiting = []
                    quantise_g(s - 1)
                else:
                    scalar_cols, vector_cols = LATE_SCALAR if scalar_is_free else (EARLY_SCALAR if s < EARLY_GROUPS else SCALAR_COLS), 0
                regroup_g(s, scalar_cols, vector_cols)
                for n, (b, m) in enumerate(waiting):
                    add_x_and_store(b, m, spare_vector=n == 0)
                waiting = []
                if scalar_cols:
                    regroup_g_scalar(s, scalar_cols)
                if 1 <= s < GROUPS - 1:
                    quantise_g(s - 1)
                if late_x is not None:
                    quantise(late_xg[late_x], x_codes[:, late_x, :], x_scales[:, late_x, :])
        b = BATCH - 1
        for c in range(EARLY_CHUNKS, CHUNKS - 1):
            for m in range(TOKEN_TILES):
                if c == 0:
                    late_banks += 1
                if late_banks % 5 in LATE_NORM:
                    out_pass(b, m, c, psum_norm, "norm")
                else:
                    out_pass(b, m, c, psum_out, "out")
        quantise_g(GROUPS - 1)
        for m in range(TOKEN_TILES):
            out_pass(b, m, CHUNKS - 1, psum_out, "out")
            add_x_and_store(b, m, spare_vector=False)
